import numpy as np
import ml_dtypes


def mxq(x, axis, fmt="e4m3"):
    dtype, down = {"e4m3": (ml_dtypes.float8_e4m3fn, 7), "e5m2": (ml_dtypes.float8_e5m2, 14)}[fmt]
    v = np.moveaxis(np.asarray(x, np.float32).astype(ml_dtypes.bfloat16).astype(np.float64), axis, -1)
    blocks = v.reshape(v.shape[:-1] + (-1, 32))
    amax = np.abs(blocks).max(-1, keepdims=True)
    byte = np.maximum(np.where(amax > 0, np.frexp(amax)[1] - 1 + 127, 0) - down, 1)
    scale = np.exp2(byte - 127.0)
    codes = (blocks / scale).astype(np.float32).astype(dtype).astype(np.float64)
    return np.moveaxis((codes * scale).reshape(v.shape), -1, axis)


WIDE = False


def mx_kscale(k):
    if not WIDE:
        return np.ones(k)
    levels = np.array([10, -10, 5, -5, 0])
    a = np.random.permutation(np.resize(levels, k // 512 * 4)).reshape(k // 512, 4)
    idx = np.arange(k)
    return np.exp2(a[idx // 512, idx % 128 // 32])


BF16 = ml_dtypes.bfloat16


def bf(x):
    return np.asarray(x, np.float32).astype(BF16)


def f64(x):
    return np.asarray(x).astype(np.float64)


B, T, C, HQ, HKV, HD = 4, 256, 2048, 16, 4, 128
E = HQ * HD


def sigmoid(v):
    return 1.0 / (1.0 + np.exp(-v))


def setup_inputs():
    t = mx_kscale(E)
    return {"attn": bf(np.random.standard_normal((B, T, HQ, HD)) * 0.5 * t.reshape(HQ, HD)),
            "Wg": bf(np.random.standard_normal((HD, HD)) * 2.0 / np.sqrt(HD) / t.max()),
            "bg": bf(np.random.standard_normal(HD) * 0.3),
            "Wo": bf(np.random.standard_normal((C, E)) * 2.0 / np.sqrt(E) / t),
            "bo": bf(np.random.standard_normal(C) * 0.1)}


def reference(attn, Wg, bg, Wo, bo):
    a = f64(attn)
    gate = sigmoid(a @ f64(Wg).T + f64(bg))
    h = (a * gate).reshape(B * T, E)
    return ((mxq(h, 1, "e4m3") @ mxq(f64(Wo), 1, "e4m3").T) + f64(bo)).reshape(B, T, C)

@@ -1,0 +1,216 @@
+from contextlib import ExitStack
+
+import concourse.mybir as mybir
+from concourse.masks import make_identity
+
+BF16 = mybir.dt.bfloat16
+F32 = mybir.dt.float32
+U32 = mybir.dt.uint32
+U8 = mybir.dt.uint8
+FP8X4 = mybir.dt.float8_e4m3fn_x4
+SIGMOID = mybir.ActivationFunctionType.Sigmoid
+MULT = mybir.AluOpType.mult
+ADD = mybir.AluOpType.add
+
+P = 128
+TOKENS = 4 * 256
+HEADS = 16
+E = HEADS * P
+C = 2048
+PACK = 4
+K_PASS = P * PACK
+PASSES = E // K_PASS
+TOKEN_TILES = TOKENS // P
+CHUNK = 512
+CHUNKS = C // CHUNK
+ROW_TILES = CHUNK // P
+BANK_BLOCKS = 8
+FIRST = 4
+
+FLOPS = 2 * TOKENS * E * C + 2 * TOKENS * HEADS * P * P
+
+
+def tile_gqaselfattention_pb_kernel(tc, attn, Wg, bg, Wo, bo, out):
+    nc = tc.nc
+    attn_rows = attn.rearrange("b t h d -> (b t) (h d)")
+    out_rows = out.rearrange("b t c -> (b t) c")
+
+    with ExitStack() as ctx:
+        keep = ctx.enter_context(tc.tile_pool(name="keep", bufs=1))
+        feat_pool = ctx.enter_context(tc.tile_pool(name="feat", bufs=3))
+        gate_pool = ctx.enter_context(tc.tile_pool(name="gate", bufs=4))
+        gated_pool = ctx.enter_context(tc.tile_pool(name="gated", bufs=2))
+        grouped_pool = ctx.enter_context(tc.tile_pool(name="grouped", bufs=3))
+        result_pool = ctx.enter_context(tc.tile_pool(name="result", bufs=6))
+        block_banks = ctx.enter_context(tc.psum_pool(name="blocks", bufs=4))
+        gate_banks = ctx.enter_context(tc.psum_pool(name="gates", bufs=2))
+        product_banks = ctx.enter_context(tc.psum_pool(name="products", bufs=2))
+        ctx.enter_context(tc.manual_schedule())
+
+        tokens_in = keep.tile([P, TOKEN_TILES, E], BF16)
+        wo_in = keep.tile([P, CHUNKS, ROW_TILES, E], BF16)
+        bo_all = keep.tile([P, C], BF16)
+        wg_in = keep.tile([P, P], BF16)
+        bg_in = keep.tile([P, P], BF16)
+
+        def load_tokens(m):
+            nc.sync.dma_start(out=tokens_in[:, m, :], in_=attn_rows[m * P : (m + 1) * P, :])
+
+        def load_wo(n):
+            rows = Wo[n * CHUNK : (n + 1) * CHUNK, :]
+            nc.sync.dma_start(out=wo_in[:, n, :, :], in_=rows.rearrange("(j p) e -> p j e", p=P))
+
+        nc.vector.memset(bg_in[:], 0.0)
+        nc.scalar.dma_start(out=wg_in[:], in_=Wg)
+        nc.scalar.dma_start(out=bg_in[0:1, :], in_=bg.rearrange("(o f) -> o f", o=1))
+        for m in range(FIRST):
+            load_tokens(m)
+        load_wo(0)
+        nc.sync.dma_start(out=bo_all[:], in_=bo.partition_broadcast(P))
+        for n in range(1, CHUNKS):
+            load_wo(n)
+        for m in range(FIRST, TOKEN_TILES):
+            load_tokens(m)
+
+        ident = keep.tile([P, P], BF16)
+        make_identity(nc, ident[:])
+        wg_t = keep.tile([P, P], BF16)
+        bg_col = keep.tile([P, 1], F32)
+        setup = block_banks.tile([P, BANK_BLOCKS * P], BF16, tag="blocks")
+        nc.tensor.transpose(out=setup[:, 0:P], in_=wg_in[:], identity=ident[:])
+        nc.tensor.transpose(out=setup[:, P : 2 * P], in_=bg_in[:], identity=ident[:])
+        nc.scalar.copy(out=wg_t[:], in_=setup[:, 0:P])
+        nc.scalar.copy(out=bg_col[:], in_=setup[:, P : P + 1])
+
+        h_codes = keep.tile([P, TOKEN_TILES, PASSES * P], U32, align_bytes=64)
+        h_scales = keep.tile([P, TOKEN_TILES, PASSES * P], U8, align_bytes=64)
+        wo_codes = keep.tile([P, PASSES, C], U32, align_bytes=64)
+        wo_scales = keep.tile([P, PASSES, C], U8, align_bytes=64)
+
+        feats_of = {}
+        gated_of = {}
+        grouped_of = {}
+
+        def transpose_tokens(m):
+            feats = feat_pool.tile([P, E], BF16, name="feats")
+            feats_of[m] = feats
+            for half in range(2):
+                bank = block_banks.tile([P, BANK_BLOCKS * P], BF16, name="bank", tag="blocks")
+                for i in range(BANK_BLOCKS):
+                    head = half * BANK_BLOCKS + i
+                    nc.tensor.transpose(
+                        out=bank[:, i * P : (i + 1) * P],
+                        in_=tokens_in[:, m, head * P : (head + 1) * P],
+                        identity=ident[:],
+                    )
+                dst = feats[:, half * BANK_BLOCKS * P : (half + 1) * BANK_BLOCKS * P]
+                if half == 0:
+                    nc.scalar.copy(out=dst, in_=bank[:])
+                else:
+                    nc.vector.tensor_copy(out=dst, in_=bank[:])
+
+        def gate_tokens(m, g):
+            if g == 0:
+                gated_of[m] = gated_pool.tile([P, PASSES, P, PACK], BF16, name="gated", align_bytes=64)
+            four_heads = feats_of[m][:, g * K_PASS : (g + 1) * K_PASS]
+            z = gate_banks.tile([P, K_PASS], F32, name="z")
+            nc.tensor.matmul(out=z[:], lhsT=wg_t[:], rhs=four_heads, start=True, stop=True)
+            gate = gate_pool.tile([P, P, PACK], F32, name="gate")
+            nc.scalar.activation(
+                out=gate[:],
+                in_=z[:].rearrange("p (t r) -> p r t", t=PACK),
+                func=SIGMOID,
+                bias=bg_col[:, 0:1],
+            )
+            nc.vector.tensor_tensor(
+                out=gated_of[m][:, g, :, :],
+                in0=gate[:],
+                in1=four_heads.rearrange("p (t r) -> p r t", t=PACK),
+                op=MULT,
+            )
+
+        def quantise_tokens(m):
+            nc.vector.quantize_mx(
+                out=h_codes[:, m, :].bitcast(FP8X4),
+                scales=h_scales[:, m, :],
+                in_=gated_of[m][:].rearrange("p g r t -> p (g r t)"),
+            )
+
+        def transpose_wo(n, g):
+            grouped = grouped_pool.tile([P, CHUNK, PACK], BF16, name="grouped", align_bytes=64)
+            grouped_of[(n, g)] = grouped
+            for half in range(2):
+                bank = block_banks.tile([P, BANK_BLOCKS * P], BF16, name="bank", tag="blocks")
+                for j in range(2):
+                    for t in range(PACK):
+                        first = g * K_PASS + t * P
+                        nc.tensor.transpose(
+                            out=bank[:, (j * PACK + t) * P : (j * PACK + t + 1) * P],
+                            in_=wo_in[:, n, 2 * half + j, first : first + P],
+                            identity=ident[:],
+                        )
+                dst = grouped[:, half * 2 * P : (half + 1) * 2 * P, :].rearrange("p (j c) t -> p j c t", j=2)
+                src = bank[:].rearrange("p (j t c) -> p j c t", j=2, t=PACK)
+                if half == 1 and g % 2 == 1:
+                    nc.vector.tensor_copy(out=dst, in_=src)
+                else:
+                    nc.scalar.copy(out=dst, in_=src)
+
+        def quantise_wo(n, g):
+            cols = slice(n * CHUNK, (n + 1) * CHUNK)
+            nc.vector.quantize_mx(
+                out=wo_codes[:, g, cols].bitcast(FP8X4),
+                scales=wo_scales[:, g, cols],
+                in_=grouped_of[(n, g)][:].rearrange("p c t -> p (c t)"),
+            )
+
+        def product(m, n):
+            cols = slice(n * CHUNK, (n + 1) * CHUNK)
+            acc = product_banks.tile([P, CHUNK], F32, name="acc")
+            for g in range(PASSES):
+                toks = slice(g * P, (g + 1) * P)
+                nc.tensor.matmul_mx(
+                    out=acc[:],
+                    lhsT=h_codes[:, m, toks].bitcast(FP8X4),
+                    lhsT_scale=h_scales[:, m, toks],
+                    rhs=wo_codes[:, g, cols].bitcast(FP8X4),
+                    rhs_scale=wo_scales[:, g, cols],
+                    start=(g == 0),
+                    stop=(g == PASSES - 1),
+                )
+            result = result_pool.tile([P, CHUNK], F32, name="result")
+            nc.vector.tensor_tensor(out=result[:], in0=acc[:], in1=bo_all[:, cols], op=ADD)
+            nc.sync.dma_start(out=out_rows[m * P : (m + 1) * P, cols], in_=result[:])
+
+        transpose_tokens(0)
+        for m in range(FIRST):
+            if m + 1 < FIRST:
+                transpose_tokens(m + 1)
+            for g in range(PASSES):
+                gate_tokens(m, g)
+            quantise_tokens(m)
+
+        for n in range(CHUNKS):
+            for g in range(PASSES):
+                transpose_wo(n, g)
+                if n > 0:
+                    product(g, n - 1)
+                quantise_wo(n, g)
+        transpose_tokens(FIRST)
+
+        ready = [(m, CHUNKS - 1) for m in range(FIRST)]
+        for m in range(FIRST, TOKEN_TILES):
+            gate_tokens(m, 0)
+            gate_tokens(m, 1)
+            product(*ready[0])
+            gate_tokens(m, 2)
+            gate_tokens(m, 3)
+            product(*ready[1])
+            if m + 1 < TOKEN_TILES:
+                transpose_tokens(m + 1)
+            product(*ready[2])
+            quantise_tokens(m)
+            product(*ready[3])
+            ready = [(m, n) for n in range(CHUNKS)]
+        for m, n in ready:
+            product(m, n)

@@ -45,7 +45,6 @@ def tile_gqaselfattention_pb_kernel(tc, attn, Wg, bg, Wo, bo, out):
         block_banks = ctx.enter_context(tc.psum_pool(name="blocks", bufs=4))
         gate_banks = ctx.enter_context(tc.psum_pool(name="gates", bufs=2))
         product_banks = ctx.enter_context(tc.psum_pool(name="products", bufs=2))
-        ctx.enter_context(tc.manual_schedule())
 
         tokens_in = keep.tile([P, TOKEN_TILES, E], BF16)
         wo_in = keep.tile([P, CHUNKS, ROW_TILES, E], BF16)

@@ -87,14 +87,17 @@ def tile_gqaselfattention_pb_kernel(tc, attn, Wg, bg, Wo, bo, out):
         wo_scales = keep.tile([P, PASSES, C], U8, align_bytes=64)
 
         feats_of = {}
+        banks_of = {}
         gated_of = {}
         grouped_of = {}
 
         def transpose_tokens(m):
             feats = feat_pool.tile([P, E], BF16, name="feats")
             feats_of[m] = feats
+            banks_of[m] = []
             for half in range(2):
                 bank = block_banks.tile([P, BANK_BLOCKS * P], BF16, name="bank", tag="blocks")
+                banks_of[m].append(bank)
                 for i in range(BANK_BLOCKS):
                     head = half * BANK_BLOCKS + i
                     nc.tensor.transpose(
@@ -121,10 +124,11 @@ def tile_gqaselfattention_pb_kernel(tc, attn, Wg, bg, Wo, bo, out):
                 func=SIGMOID,
                 bias=bg_col[:, 0:1],
             )
+            in_bank = banks_of[m][g // 2][:, (g % 2) * K_PASS : (g % 2 + 1) * K_PASS]
             nc.vector.tensor_tensor(
                 out=gated_of[m][:, g, :, :],
                 in0=gate[:],
-                in1=four_heads.rearrange("p (t r) -> p r t", t=PACK),
+                in1=in_bank.rearrange("p (t r) -> p r t", t=PACK),
                 op=MULT,
             )
 

@@ -23,11 +23,24 @@ PASSES = E // K_PASS
 TOKEN_TILES = TOKENS // P
 CHUNK = 512
 CHUNKS = C // CHUNK
-ROW_TILES = CHUNK // P
 BANK_BLOCKS = 8
+BLOCK_BANKS = 4
+PAIRS = HEADS // 2
+ROWS_HELD = P // PAIRS
+SLAB = 256
+SLABS = C // SLAB
+CHUNK_SLABS = CHUNK // SLAB
+SLAB_GROUPS = SLAB // ROWS_HELD
+BANK_GROUPS = BANK_BLOCKS // 2
+BANK_ROWS = BANK_GROUPS * ROWS_HELD
 FIRST = 4
+SLAB_PRODUCTS = FIRST // CHUNK_SLABS
 
 FLOPS = 2 * TOKENS * E * C + 2 * TOKENS * HEADS * P * P
+
+
+def head_of(g, t):
+    return PACK * g + 2 * (t % 2) + t // 2
 
 
 def tile_gqaselfattention_pb_kernel(tc, attn, Wg, bg, Wo, bo, out):
@@ -41,13 +54,13 @@ def tile_gqaselfattention_pb_kernel(tc, attn, Wg, bg, Wo, bo, out):
         gate_pool = ctx.enter_context(tc.tile_pool(name="gate", bufs=4))
         gated_pool = ctx.enter_context(tc.tile_pool(name="gated", bufs=2))
         grouped_pool = ctx.enter_context(tc.tile_pool(name="grouped", bufs=3))
-        result_pool = ctx.enter_context(tc.tile_pool(name="result", bufs=6))
-        block_banks = ctx.enter_context(tc.psum_pool(name="blocks", bufs=4))
+        result_pool = ctx.enter_context(tc.tile_pool(name="result", bufs=8))
+        block_banks = ctx.enter_context(tc.psum_pool(name="blocks", bufs=BLOCK_BANKS))
         gate_banks = ctx.enter_context(tc.psum_pool(name="gates", bufs=2))
         product_banks = ctx.enter_context(tc.psum_pool(name="products", bufs=2))
 
         tokens_in = keep.tile([P, TOKEN_TILES, E], BF16)
-        wo_in = keep.tile([P, CHUNKS, ROW_TILES, E], BF16)
+        wo_in = keep.tile([P, SLABS, SLAB_GROUPS, 2 * P], BF16)
         bo_all = keep.tile([P, C], BF16)
         wg_in = keep.tile([P, P], BF16)
         bg_in = keep.tile([P, P], BF16)
@@ -55,31 +68,41 @@ def tile_gqaselfattention_pb_kernel(tc, attn, Wg, bg, Wo, bo, out):
         def load_tokens(m):
             nc.sync.dma_start(out=tokens_in[:, m, :], in_=attn_rows[m * P : (m + 1) * P, :])
 
-        def load_wo(n):
-            rows = Wo[n * CHUNK : (n + 1) * CHUNK, :]
-            nc.sync.dma_start(out=wo_in[:, n, :, :], in_=rows.rearrange("(j p) e -> p j e", p=P))
+        def load_wo(s):
+            rows = Wo[s * SLAB : (s + 1) * SLAB, :]
+            nc.sync.dma_start(
+                out=wo_in[:, s, :, :],
+                in_=rows.rearrange("(b r) (pair f) -> (r pair) b f", r=ROWS_HELD, pair=PAIRS),
+            )
 
         nc.vector.memset(bg_in[:], 0.0)
         nc.scalar.dma_start(out=wg_in[:], in_=Wg)
         nc.scalar.dma_start(out=bg_in[0:1, :], in_=bg.rearrange("(o f) -> o f", o=1))
         for m in range(FIRST):
             load_tokens(m)
-        load_wo(0)
+        for s in range(CHUNK_SLABS):
+            load_wo(s)
         nc.sync.dma_start(out=bo_all[:], in_=bo.partition_broadcast(P))
-        for n in range(1, CHUNKS):
-            load_wo(n)
+        for s in range(CHUNK_SLABS, SLABS):
+            load_wo(s)
         for m in range(FIRST, TOKEN_TILES):
             load_tokens(m)
+
+        warm = keep.tile([P, 1], F32)
+        nc.vector.memset(warm[:], 0.0)
+        nc.scalar.activation(out=warm[:], in_=warm[:], func=SIGMOID)
 
         ident = keep.tile([P, P], BF16)
         make_identity(nc, ident[:])
         wg_t = keep.tile([P, P], BF16)
         bg_col = keep.tile([P, 1], F32)
-        setup = block_banks.tile([P, BANK_BLOCKS * P], BF16, tag="blocks")
-        nc.tensor.transpose(out=setup[:, 0:P], in_=wg_in[:], identity=ident[:])
-        nc.tensor.transpose(out=setup[:, P : 2 * P], in_=bg_in[:], identity=ident[:])
-        nc.scalar.copy(out=wg_t[:], in_=setup[:, 0:P])
-        nc.scalar.copy(out=bg_col[:], in_=setup[:, P : P + 1])
+
+        def set_up_gate():
+            setup = block_banks.tile([P, BANK_BLOCKS * P], BF16, name="setup", tag="blocks")
+            nc.tensor.transpose(out=setup[:, 0:P], in_=wg_in[:], identity=ident[:])
+            nc.tensor.transpose(out=setup[:, P : 2 * P], in_=bg_in[:], identity=ident[:])
+            nc.scalar.copy(out=wg_t[:], in_=setup[:, 0:P])
+            nc.scalar.copy(out=bg_col[:], in_=setup[:, P : P + 1])
 
         h_codes = keep.tile([P, TOKEN_TILES, PASSES * P], U32, align_bytes=64)
         h_scales = keep.tile([P, TOKEN_TILES, PASSES * P], U8, align_bytes=64)
@@ -87,29 +110,27 @@ def tile_gqaselfattention_pb_kernel(tc, attn, Wg, bg, Wo, bo, out):
         wo_scales = keep.tile([P, PASSES, C], U8, align_bytes=64)
 
         feats_of = {}
-        banks_of = {}
         gated_of = {}
         grouped_of = {}
 
         def transpose_tokens(m):
             feats = feat_pool.tile([P, E], BF16, name="feats")
             feats_of[m] = feats
-            banks_of[m] = []
             for half in range(2):
                 bank = block_banks.tile([P, BANK_BLOCKS * P], BF16, name="bank", tag="blocks")
-                banks_of[m].append(bank)
                 for i in range(BANK_BLOCKS):
-                    head = half * BANK_BLOCKS + i
+                    place = half * BANK_BLOCKS + i
+                    head = head_of(place // PACK, place % PACK)
                     nc.tensor.transpose(
                         out=bank[:, i * P : (i + 1) * P],
                         in_=tokens_in[:, m, head * P : (head + 1) * P],
                         identity=ident[:],
                     )
                 dst = feats[:, half * BANK_BLOCKS * P : (half + 1) * BANK_BLOCKS * P]
-                if half == 0:
-                    nc.scalar.copy(out=dst, in_=bank[:])
-                else:
+                if half == 1 and m < FIRST:
                     nc.vector.tensor_copy(out=dst, in_=bank[:])
+                else:
+                    nc.scalar.copy(out=dst, in_=bank[:])
 
         def gate_tokens(m, g):
             if g == 0:
@@ -124,11 +145,10 @@ def tile_gqaselfattention_pb_kernel(tc, attn, Wg, bg, Wo, bo, out):
                 func=SIGMOID,
                 bias=bg_col[:, 0:1],
             )
-            in_bank = banks_of[m][g // 2][:, (g % 2) * K_PASS : (g % 2 + 1) * K_PASS]
             nc.vector.tensor_tensor(
                 out=gated_of[m][:, g, :, :],
                 in0=gate[:],
-                in1=in_bank.rearrange("p (t r) -> p r t", t=PACK),
+                in1=four_heads.rearrange("p (t r) -> p r t", t=PACK),
                 op=MULT,
             )
 
@@ -139,33 +159,33 @@ def tile_gqaselfattention_pb_kernel(tc, attn, Wg, bg, Wo, bo, out):
                 in_=gated_of[m][:].rearrange("p g r t -> p (g r t)"),
             )
 
-        def transpose_wo(n, g):
-            grouped = grouped_pool.tile([P, CHUNK, PACK], BF16, name="grouped", align_bytes=64)
-            grouped_of[(n, g)] = grouped
-            for half in range(2):
+        def transpose_wo(s):
+            grouped = grouped_pool.tile([P, PASSES * SLAB * PACK], BF16, name="grouped", align_bytes=64)
+            grouped_of[s] = grouped
+            grouped_words = grouped[:].bitcast(F32).rearrange("p (g c a) -> p g c a", g=PASSES, a=2)
+            for i in range(BLOCK_BANKS):
                 bank = block_banks.tile([P, BANK_BLOCKS * P], BF16, name="bank", tag="blocks")
-                for j in range(2):
-                    for t in range(PACK):
-                        first = g * K_PASS + t * P
+                for a in range(2):
+                    for b in range(BANK_GROUPS):
+                        place = a * BANK_GROUPS + b
                         nc.tensor.transpose(
-                            out=bank[:, (j * PACK + t) * P : (j * PACK + t + 1) * P],
-                            in_=wo_in[:, n, 2 * half + j, first : first + P],
+                            out=bank[:, place * P : (place + 1) * P],
+                            in_=wo_in[:, s, i * BANK_GROUPS + b, a * P : (a + 1) * P],
                             identity=ident[:],
                         )
-                dst = grouped[:, half * 2 * P : (half + 1) * 2 * P, :].rearrange("p (j c) t -> p j c t", j=2)
-                src = bank[:].rearrange("p (j t c) -> p j c t", j=2, t=PACK)
-                if half == 1 and g % 2 == 1:
-                    nc.vector.tensor_copy(out=dst, in_=src)
-                else:
-                    nc.scalar.copy(out=dst, in_=src)
+                nc.scalar.copy(
+                    out=grouped_words[:, :, i * BANK_ROWS : (i + 1) * BANK_ROWS, :],
+                    in_=bank[:].bitcast(F32).rearrange("p (a c g) -> p g c a", a=2, g=PASSES),
+                )
 
-        def quantise_wo(n, g):
-            cols = slice(n * CHUNK, (n + 1) * CHUNK)
-            nc.vector.quantize_mx(
-                out=wo_codes[:, g, cols].bitcast(FP8X4),
-                scales=wo_scales[:, g, cols],
-                in_=grouped_of[(n, g)][:].rearrange("p c t -> p (c t)"),
-            )
+        def quantise_wo(s):
+            cols = slice(s * SLAB, (s + 1) * SLAB)
+            for g in range(PASSES):
+                nc.vector.quantize_mx(
+                    out=wo_codes[:, g, cols].bitcast(FP8X4),
+                    scales=wo_scales[:, g, cols],
+                    in_=grouped_of[s][:, g * SLAB * PACK : (g + 1) * SLAB * PACK],
+                )
 
         def product(m, n):
             cols = slice(n * CHUNK, (n + 1) * CHUNK)
@@ -186,19 +206,25 @@ def tile_gqaselfattention_pb_kernel(tc, attn, Wg, bg, Wo, bo, out):
             nc.sync.dma_start(out=out_rows[m * P : (m + 1) * P, cols], in_=result[:])
 
         transpose_tokens(0)
+        set_up_gate()
         for m in range(FIRST):
+            gate_tokens(m, 0)
+            gate_tokens(m, 1)
+            if m > 0:
+                quantise_tokens(m - 1)
             if m + 1 < FIRST:
                 transpose_tokens(m + 1)
-            for g in range(PASSES):
-                gate_tokens(m, g)
-            quantise_tokens(m)
+            gate_tokens(m, 2)
+            gate_tokens(m, 3)
 
-        for n in range(CHUNKS):
-            for g in range(PASSES):
-                transpose_wo(n, g)
-                if n > 0:
-                    product(g, n - 1)
-                quantise_wo(n, g)
+        for s in range(SLABS):
+            transpose_wo(s)
+            if s == 0:
+                quantise_tokens(FIRST - 1)
+            if s >= CHUNK_SLABS:
+                for i in range(SLAB_PRODUCTS):
+                    product((s % CHUNK_SLABS) * SLAB_PRODUCTS + i, s // CHUNK_SLABS - 1)
+            quantise_wo(s)
         transpose_tokens(FIRST)
 
         ready = [(m, CHUNKS - 1) for m in range(FIRST)]

@@ -23,24 +23,20 @@ PASSES = E // K_PASS
 TOKEN_TILES = TOKENS // P
 CHUNK = 512
 CHUNKS = C // CHUNK
-BANK_BLOCKS = 8
-BLOCK_BANKS = 4
 PAIRS = HEADS // 2
-ROWS_HELD = P // PAIRS
-SLAB = 256
+GROUP = P // PAIRS
+BANK_BLOCKS = 8
+BANK_GROUPS = BANK_BLOCKS // 2
+BANK_ROWS = BANK_GROUPS * GROUP
+BLOCK_BANKS = 4
+TILE_BANKS = P // BANK_ROWS
+SLAB = BLOCK_BANKS * BANK_ROWS
 SLABS = C // SLAB
 CHUNK_SLABS = CHUNK // SLAB
-SLAB_GROUPS = SLAB // ROWS_HELD
-BANK_GROUPS = BANK_BLOCKS // 2
-BANK_ROWS = BANK_GROUPS * ROWS_HELD
 FIRST = 4
 SLAB_PRODUCTS = FIRST // CHUNK_SLABS
 
 FLOPS = 2 * TOKENS * E * C + 2 * TOKENS * HEADS * P * P
-
-
-def head_of(g, t):
-    return PACK * g + 2 * (t % 2) + t // 2
 
 
 def tile_gqaselfattention_pb_kernel(tc, attn, Wg, bg, Wo, bo, out):
@@ -59,21 +55,23 @@ def tile_gqaselfattention_pb_kernel(tc, attn, Wg, bg, Wo, bo, out):
         gate_banks = ctx.enter_context(tc.psum_pool(name="gates", bufs=2))
         product_banks = ctx.enter_context(tc.psum_pool(name="products", bufs=2))
 
-        tokens_in = keep.tile([P, TOKEN_TILES, E], BF16)
-        wo_in = keep.tile([P, SLABS, SLAB_GROUPS, 2 * P], BF16)
+        tokens_in = keep.tile([P, TOKEN_TILES, P // GROUP, 2 * P], BF16)
+        wo_in = keep.tile([P, SLABS, SLAB // GROUP, 2 * P], BF16)
         bo_all = keep.tile([P, C], BF16)
         wg_in = keep.tile([P, P], BF16)
         bg_in = keep.tile([P, P], BF16)
 
+        def load_rows(dst, rows):
+            nc.sync.dma_start(out=dst, in_=rows.rearrange("(b r) (pair f) -> (r pair) b f", r=GROUP, pair=PAIRS))
+
         def load_tokens(m):
-            nc.sync.dma_start(out=tokens_in[:, m, :], in_=attn_rows[m * P : (m + 1) * P, :])
+            for i in range(TILE_BANKS):
+                groups = slice(i * BANK_GROUPS, (i + 1) * BANK_GROUPS)
+                first = m * P + i * BANK_ROWS
+                load_rows(tokens_in[:, m, groups, :], attn_rows[first : first + BANK_ROWS, :])
 
         def load_wo(s):
-            rows = Wo[s * SLAB : (s + 1) * SLAB, :]
-            nc.sync.dma_start(
-                out=wo_in[:, s, :, :],
-                in_=rows.rearrange("(b r) (pair f) -> (r pair) b f", r=ROWS_HELD, pair=PAIRS),
-            )
+            load_rows(wo_in[:, s, :, :], Wo[s * SLAB : (s + 1) * SLAB, :])
 
         nc.vector.memset(bg_in[:], 0.0)
         nc.scalar.dma_start(out=wg_in[:], in_=Wg)
@@ -113,70 +111,55 @@ def tile_gqaselfattention_pb_kernel(tc, attn, Wg, bg, Wo, bo, out):
         gated_of = {}
         grouped_of = {}
 
-        def transpose_tokens(m):
-            feats = feat_pool.tile([P, E], BF16, name="feats")
-            feats_of[m] = feats
-            for half in range(2):
-                bank = block_banks.tile([P, BANK_BLOCKS * P], BF16, name="bank", tag="blocks")
-                for i in range(BANK_BLOCKS):
-                    place = half * BANK_BLOCKS + i
-                    head = head_of(place // PACK, place % PACK)
-                    nc.tensor.transpose(
-                        out=bank[:, i * P : (i + 1) * P],
-                        in_=tokens_in[:, m, head * P : (head + 1) * P],
-                        identity=ident[:],
-                    )
-                dst = feats[:, half * BANK_BLOCKS * P : (half + 1) * BANK_BLOCKS * P]
-                if half == 1 and m < FIRST:
-                    nc.vector.tensor_copy(out=dst, in_=bank[:])
-                else:
-                    nc.scalar.copy(out=dst, in_=bank[:])
-
-        def gate_tokens(m, g):
-            if g == 0:
-                gated_of[m] = gated_pool.tile([P, PASSES, P, PACK], BF16, name="gated", align_bytes=64)
-            four_heads = feats_of[m][:, g * K_PASS : (g + 1) * K_PASS]
-            z = gate_banks.tile([P, K_PASS], F32, name="z")
-            nc.tensor.matmul(out=z[:], lhsT=wg_t[:], rhs=four_heads, start=True, stop=True)
-            gate = gate_pool.tile([P, P, PACK], F32, name="gate")
-            nc.scalar.activation(
-                out=gate[:],
-                in_=z[:].rearrange("p (t r) -> p r t", t=PACK),
-                func=SIGMOID,
-                bias=bg_col[:, 0:1],
-            )
-            nc.vector.tensor_tensor(
-                out=gated_of[m][:, g, :, :],
-                in0=gate[:],
-                in1=four_heads.rearrange("p (t r) -> p r t", t=PACK),
-                op=MULT,
-            )
-
-        def quantise_tokens(m):
-            nc.vector.quantize_mx(
-                out=h_codes[:, m, :].bitcast(FP8X4),
-                scales=h_scales[:, m, :],
-                in_=gated_of[m][:].rearrange("p g r t -> p (g r t)"),
-            )
-
-        def transpose_wo(s):
-            grouped = grouped_pool.tile([P, PASSES * SLAB * PACK], BF16, name="grouped", align_bytes=64)
-            grouped_of[s] = grouped
-            grouped_words = grouped[:].bitcast(F32).rearrange("p (g c a) -> p g c a", g=PASSES, a=2)
-            for i in range(BLOCK_BANKS):
+        def transpose_rows(loaded, banks, regrouped, vector_helps):
+            words = regrouped[:].bitcast(F32).rearrange("p (g c a) -> p g c a", g=PASSES, a=2)
+            for i in range(banks):
                 bank = block_banks.tile([P, BANK_BLOCKS * P], BF16, name="bank", tag="blocks")
                 for a in range(2):
                     for b in range(BANK_GROUPS):
                         place = a * BANK_GROUPS + b
                         nc.tensor.transpose(
                             out=bank[:, place * P : (place + 1) * P],
-                            in_=wo_in[:, s, i * BANK_GROUPS + b, a * P : (a + 1) * P],
+                            in_=loaded[:, i * BANK_GROUPS + b, a * P : (a + 1) * P],
                             identity=ident[:],
                         )
-                nc.scalar.copy(
-                    out=grouped_words[:, :, i * BANK_ROWS : (i + 1) * BANK_ROWS, :],
+                copy_out = nc.vector.tensor_copy if vector_helps and i == banks - 1 else nc.scalar.copy
+                copy_out(
+                    out=words[:, :, i * BANK_ROWS : (i + 1) * BANK_ROWS, :],
                     in_=bank[:].bitcast(F32).rearrange("p (a c g) -> p g c a", a=2, g=PASSES),
                 )
+
+        def transpose_tokens(m):
+            feats_of[m] = feat_pool.tile([P, PASSES * K_PASS], BF16, name="feats")
+            transpose_rows(tokens_in[:, m, :, :], TILE_BANKS, feats_of[m], m < FIRST)
+
+        def gate_tokens(m, i, j):
+            if i == 0 and j == 0:
+                gated_of[m] = gated_pool.tile([P, PASSES * K_PASS], BF16, name="gated", align_bytes=64)
+            passes = slice(2 * j, 2 * j + 2)
+            cols = slice(i * BANK_ROWS * PACK, (i + 1) * BANK_ROWS * PACK)
+            a_t = feats_of[m][:].rearrange("p (g c) -> p g c", g=PASSES)[:, passes, cols]
+            h_t = gated_of[m][:].rearrange("p (g c) -> p g c", g=PASSES)[:, passes, cols]
+            z = gate_banks.tile([P, K_PASS], F32, name="z")
+            nc.tensor.matmul(
+                out=z[:].rearrange("p (g c) -> p g c", g=2), lhsT=wg_t[:], rhs=a_t, start=True, stop=True
+            )
+            gate = gate_pool.tile([P, K_PASS], F32, name="gate")
+            nc.scalar.activation(out=gate[:], in_=z[:], func=SIGMOID, bias=bg_col[:, 0:1])
+            nc.vector.tensor_tensor(out=h_t, in0=gate[:].rearrange("p (g c) -> p g c", g=2), in1=a_t, op=MULT)
+
+        def gate_half(m, i):
+            for j in range(PASSES // 2):
+                gate_tokens(m, i, j)
+
+        def quantise_tokens(m):
+            nc.vector.quantize_mx(
+                out=h_codes[:, m, :].bitcast(FP8X4), scales=h_scales[:, m, :], in_=gated_of[m][:]
+            )
+
+        def transpose_wo(s):
+            grouped_of[s] = grouped_pool.tile([P, PASSES * SLAB * PACK], BF16, name="grouped", align_bytes=64)
+            transpose_rows(wo_in[:, s, :, :], BLOCK_BANKS, grouped_of[s], False)
 
         def quantise_wo(s):
             cols = slice(s * SLAB, (s + 1) * SLAB)
@@ -208,14 +191,12 @@ def tile_gqaselfattention_pb_kernel(tc, attn, Wg, bg, Wo, bo, out):
         transpose_tokens(0)
         set_up_gate()
         for m in range(FIRST):
-            gate_tokens(m, 0)
-            gate_tokens(m, 1)
+            gate_half(m, 0)
             if m > 0:
                 quantise_tokens(m - 1)
             if m + 1 < FIRST:
                 transpose_tokens(m + 1)
-            gate_tokens(m, 2)
-            gate_tokens(m, 3)
+            gate_half(m, 1)
 
         for s in range(SLABS):
             transpose_wo(s)
@@ -229,11 +210,9 @@ def tile_gqaselfattention_pb_kernel(tc, attn, Wg, bg, Wo, bo, out):
 
         ready = [(m, CHUNKS - 1) for m in range(FIRST)]
         for m in range(FIRST, TOKEN_TILES):
-            gate_tokens(m, 0)
-            gate_tokens(m, 1)
+            gate_half(m, 0)
             product(*ready[0])
-            gate_tokens(m, 2)
-            gate_tokens(m, 3)
+            gate_half(m, 1)
             product(*ready[1])
             if m + 1 < TOKEN_TILES:
                 transpose_tokens(m + 1)

@@ -51,9 +51,12 @@ def tile_gqaselfattention_pb_kernel(tc, attn, Wg, bg, Wo, bo, out):
         gated_pool = ctx.enter_context(tc.tile_pool(name="gated", bufs=2))
         grouped_pool = ctx.enter_context(tc.tile_pool(name="grouped", bufs=3))
         result_pool = ctx.enter_context(tc.tile_pool(name="result", bufs=8))
-        block_banks = ctx.enter_context(tc.psum_pool(name="blocks", bufs=BLOCK_BANKS))
-        gate_banks = ctx.enter_context(tc.psum_pool(name="gates", bufs=2))
-        product_banks = ctx.enter_context(tc.psum_pool(name="products", bufs=2))
+
+        psum_of = {}
+
+        def divide_psum(stack, when, blocks, gates, products):
+            for what, banks in (("blocks", blocks), ("gates", gates), ("products", products)):
+                psum_of[what] = stack.enter_context(tc.psum_pool(name=when + what, bufs=banks, reuse_waits="tile"))
 
         tokens_in = keep.tile([P, TOKEN_TILES, P // GROUP, 2 * P], BF16)
         wo_in = keep.tile([P, SLABS, SLAB // GROUP, 2 * P], BF16)
@@ -96,7 +99,7 @@ def tile_gqaselfattention_pb_kernel(tc, attn, Wg, bg, Wo, bo, out):
         bg_col = keep.tile([P, 1], F32)
 
         def set_up_gate():
-            setup = block_banks.tile([P, BANK_BLOCKS * P], BF16, name="setup", tag="blocks")
+            setup = psum_of["blocks"].tile([P, BANK_BLOCKS * P], BF16, name="setup", tag="blocks")
             nc.tensor.transpose(out=setup[:, 0:P], in_=wg_in[:], identity=ident[:])
             nc.tensor.transpose(out=setup[:, P : 2 * P], in_=bg_in[:], identity=ident[:])
             nc.scalar.copy(out=wg_t[:], in_=setup[:, 0:P])
@@ -114,7 +117,7 @@ def tile_gqaselfattention_pb_kernel(tc, attn, Wg, bg, Wo, bo, out):
         def transpose_rows(loaded, banks, regrouped, vector_helps):
             words = regrouped[:].bitcast(F32).rearrange("p (g c a) -> p g c a", g=PASSES, a=2)
             for i in range(banks):
-                bank = block_banks.tile([P, BANK_BLOCKS * P], BF16, name="bank", tag="blocks")
+                bank = psum_of["blocks"].tile([P, BANK_BLOCKS * P], BF16, name="bank", tag="blocks")
                 for a in range(2):
                     for b in range(BANK_GROUPS):
                         place = a * BANK_GROUPS + b
@@ -140,7 +143,7 @@ def tile_gqaselfattention_pb_kernel(tc, attn, Wg, bg, Wo, bo, out):
             cols = slice(i * BANK_ROWS * PACK, (i + 1) * BANK_ROWS * PACK)
             a_t = feats_of[m][:].rearrange("p (g c) -> p g c", g=PASSES)[:, passes, cols]
             h_t = gated_of[m][:].rearrange("p (g c) -> p g c", g=PASSES)[:, passes, cols]
-            z = gate_banks.tile([P, K_PASS], F32, name="z")
+            z = psum_of["gates"].tile([P, K_PASS], F32, name="z")
             nc.tensor.matmul(
                 out=z[:].rearrange("p (g c) -> p g c", g=2), lhsT=wg_t[:], rhs=a_t, start=True, stop=True
             )
@@ -172,7 +175,7 @@ def tile_gqaselfattention_pb_kernel(tc, attn, Wg, bg, Wo, bo, out):
 
         def product(m, n):
             cols = slice(n * CHUNK, (n + 1) * CHUNK)
-            acc = product_banks.tile([P, CHUNK], F32, name="acc")
+            acc = psum_of["products"].tile([P, CHUNK], F32, name="acc")
             for g in range(PASSES):
                 toks = slice(g * P, (g + 1) * P)
                 nc.tensor.matmul_mx(
@@ -188,37 +191,43 @@ def tile_gqaselfattention_pb_kernel(tc, attn, Wg, bg, Wo, bo, out):
             nc.vector.tensor_tensor(out=result[:], in0=acc[:], in1=bo_all[:, cols], op=ADD)
             nc.sync.dma_start(out=out_rows[m * P : (m + 1) * P, cols], in_=result[:])
 
-        transpose_tokens(0)
-        set_up_gate()
-        for m in range(FIRST):
-            gate_half(m, 0)
-            if m > 0:
-                quantise_tokens(m - 1)
-            if m + 1 < FIRST:
-                transpose_tokens(m + 1)
-            gate_half(m, 1)
+        with ExitStack() as early:
+            divide_psum(early, "early_", BLOCK_BANKS, 2, 2)
 
-        for s in range(SLABS):
-            transpose_wo(s)
-            if s == 0:
-                quantise_tokens(FIRST - 1)
-            if s >= CHUNK_SLABS:
-                for i in range(SLAB_PRODUCTS):
-                    product((s % CHUNK_SLABS) * SLAB_PRODUCTS + i, s // CHUNK_SLABS - 1)
-            quantise_wo(s)
-        transpose_tokens(FIRST)
+            transpose_tokens(0)
+            set_up_gate()
+            for m in range(FIRST):
+                gate_half(m, 0)
+                if m > 0:
+                    quantise_tokens(m - 1)
+                if m + 1 < FIRST:
+                    transpose_tokens(m + 1)
+                gate_half(m, 1)
 
-        ready = [(m, CHUNKS - 1) for m in range(FIRST)]
-        for m in range(FIRST, TOKEN_TILES):
-            gate_half(m, 0)
-            product(*ready[0])
-            gate_half(m, 1)
-            product(*ready[1])
-            if m + 1 < TOKEN_TILES:
-                transpose_tokens(m + 1)
-            product(*ready[2])
-            quantise_tokens(m)
-            product(*ready[3])
-            ready = [(m, n) for n in range(CHUNKS)]
-        for m, n in ready:
-            product(m, n)
+            for s in range(SLABS):
+                transpose_wo(s)
+                if s == 0:
+                    quantise_tokens(FIRST - 1)
+                if s >= CHUNK_SLABS:
+                    for i in range(SLAB_PRODUCTS):
+                        product((s % CHUNK_SLABS) * SLAB_PRODUCTS + i, s // CHUNK_SLABS - 1)
+                quantise_wo(s)
+
+        with ExitStack() as late:
+            divide_psum(late, "late_", TILE_BANKS, 3, 3)
+
+            transpose_tokens(FIRST)
+            ready = [(m, CHUNKS - 1) for m in range(FIRST)]
+            for m in range(FIRST, TOKEN_TILES):
+                gate_half(m, 0)
+                product(*ready[0])
+                gate_half(m, 1)
+                product(*ready[1])
+                if m + 1 < TOKEN_TILES:
+                    transpose_tokens(m + 1)
+                product(*ready[2])
+                quantise_tokens(m)
+                product(*ready[3])
+                ready = [(m, n) for n in range(CHUNKS)]
+            for m, n in ready:
+                product(m, n)

from contextlib import ExitStack

import concourse.mybir as mybir
from concourse.masks import make_identity

BF16 = mybir.dt.bfloat16
F32 = mybir.dt.float32
U32 = mybir.dt.uint32
U8 = mybir.dt.uint8
FP8X4 = mybir.dt.float8_e4m3fn_x4
SIGMOID = mybir.ActivationFunctionType.Sigmoid
MULT = mybir.AluOpType.mult
ADD = mybir.AluOpType.add

P = 128
TOKENS = 4 * 256
HEADS = 16
E = HEADS * P
C = 2048
PACK = 4
K_PASS = P * PACK
PASSES = E // K_PASS
TOKEN_TILES = TOKENS // P
CHUNK = 512
CHUNKS = C // CHUNK
PAIRS = HEADS // 2
GROUP = P // PAIRS
BANK_BLOCKS = 8
BANK_GROUPS = BANK_BLOCKS // 2
BANK_ROWS = BANK_GROUPS * GROUP
BLOCK_BANKS = 4
TILE_BANKS = P // BANK_ROWS
SLAB = BLOCK_BANKS * BANK_ROWS
SLABS = C // SLAB
CHUNK_SLABS = CHUNK // SLAB
FIRST = 4
SLAB_PRODUCTS = FIRST // CHUNK_SLABS

FLOPS = 2 * TOKENS * E * C + 2 * TOKENS * HEADS * P * P


def tile_gqaselfattention_pb_kernel(tc, attn, Wg, bg, Wo, bo, out):
    nc = tc.nc
    attn_rows = attn.rearrange("b t h d -> (b t) (h d)")
    out_rows = out.rearrange("b t c -> (b t) c")

    with ExitStack() as ctx:
        keep = ctx.enter_context(tc.tile_pool(name="keep", bufs=1))
        feat_pool = ctx.enter_context(tc.tile_pool(name="feat", bufs=3))
        gate_pool = ctx.enter_context(tc.tile_pool(name="gate", bufs=4))
        gated_pool = ctx.enter_context(tc.tile_pool(name="gated", bufs=2))
        grouped_pool = ctx.enter_context(tc.tile_pool(name="grouped", bufs=3))
        result_pool = ctx.enter_context(tc.tile_pool(name="result", bufs=8))

        psum_of = {}

        def divide_psum(stack, when, blocks, gates, products):
            for what, banks in (("blocks", blocks), ("gates", gates), ("products", products)):
                psum_of[what] = stack.enter_context(tc.psum_pool(name=when + what, bufs=banks, reuse_waits="tile"))

        tokens_in = keep.tile([P, TOKEN_TILES, P // GROUP, 2 * P], BF16)
        wo_in = keep.tile([P, SLABS, SLAB // GROUP, 2 * P], BF16)
        bo_all = keep.tile([P, C], BF16)
        wg_in = keep.tile([P, P], BF16)
        bg_in = keep.tile([P, P], BF16)

        def load_rows(dst, rows):
            nc.sync.dma_start(out=dst, in_=rows.rearrange("(b r) (pair f) -> (r pair) b f", r=GROUP, pair=PAIRS))

        def load_tokens(m):
            for i in range(TILE_BANKS):
                groups = slice(i * BANK_GROUPS, (i + 1) * BANK_GROUPS)
                first = m * P + i * BANK_ROWS
                load_rows(tokens_in[:, m, groups, :], attn_rows[first : first + BANK_ROWS, :])

        def load_wo(s):
            load_rows(wo_in[:, s, :, :], Wo[s * SLAB : (s + 1) * SLAB, :])

        nc.vector.memset(bg_in[:], 0.0)
        nc.scalar.dma_start(out=wg_in[:], in_=Wg)
        nc.scalar.dma_start(out=bg_in[0:1, :], in_=bg.rearrange("(o f) -> o f", o=1))
        for m in range(FIRST):
            load_tokens(m)
        for s in range(CHUNK_SLABS):
            load_wo(s)
        nc.sync.dma_start(out=bo_all[:], in_=bo.partition_broadcast(P))
        for s in range(CHUNK_SLABS, SLABS):
            load_wo(s)
        for m in range(FIRST, TOKEN_TILES):
            load_tokens(m)

        warm = keep.tile([P, 1], F32)
        nc.vector.memset(warm[:], 0.0)
        nc.scalar.activation(out=warm[:], in_=warm[:], func=SIGMOID)

        ident = keep.tile([P, P], BF16)
        make_identity(nc, ident[:])
        wg_t = keep.tile([P, P], BF16)
        bg_col = keep.tile([P, 1], F32)

        def set_up_gate():
            setup = psum_of["blocks"].tile([P, BANK_BLOCKS * P], BF16, name="setup", tag="blocks")
            nc.tensor.transpose(out=setup[:, 0:P], in_=wg_in[:], identity=ident[:])
            nc.tensor.transpose(out=setup[:, P : 2 * P], in_=bg_in[:], identity=ident[:])
            nc.scalar.copy(out=wg_t[:], in_=setup[:, 0:P])
            nc.scalar.copy(out=bg_col[:], in_=setup[:, P : P + 1])

        h_codes = keep.tile([P, TOKEN_TILES, PASSES * P], U32, align_bytes=64)
        h_scales = keep.tile([P, TOKEN_TILES, PASSES * P], U8, align_bytes=64)
        wo_codes = keep.tile([P, PASSES, C], U32, align_bytes=64)
        wo_scales = keep.tile([P, PASSES, C], U8, align_bytes=64)

        feats_of = {}
        gated_of = {}
        grouped_of = {}

        def transpose_rows(loaded, banks, regrouped, vector_helps):
            words = regrouped[:].bitcast(F32).rearrange("p (g c a) -> p g c a", g=PASSES, a=2)
            for i in range(banks):
                bank = psum_of["blocks"].tile([P, BANK_BLOCKS * P], BF16, name="bank", tag="blocks")
                for a in range(2):
                    for b in range(BANK_GROUPS):
                        place = a * BANK_GROUPS + b
                        nc.tensor.transpose(
                            out=bank[:, place * P : (place + 1) * P],
                            in_=loaded[:, i * BANK_GROUPS + b, a * P : (a + 1) * P],
                            identity=ident[:],
                        )
                copy_out = nc.vector.tensor_copy if vector_helps and i == banks - 1 else nc.scalar.copy
                copy_out(
                    out=words[:, :, i * BANK_ROWS : (i + 1) * BANK_ROWS, :],
                    in_=bank[:].bitcast(F32).rearrange("p (a c g) -> p g c a", a=2, g=PASSES),
                )

        def transpose_tokens(m):
            feats_of[m] = feat_pool.tile([P, PASSES * K_PASS], BF16, name="feats")
            transpose_rows(tokens_in[:, m, :, :], TILE_BANKS, feats_of[m], m < FIRST)

        def gate_tokens(m, i, j):
            if i == 0 and j == 0:
                gated_of[m] = gated_pool.tile([P, PASSES * K_PASS], BF16, name="gated", align_bytes=64)
            passes = slice(2 * j, 2 * j + 2)
            cols = slice(i * BANK_ROWS * PACK, (i + 1) * BANK_ROWS * PACK)
            a_t = feats_of[m][:].rearrange("p (g c) -> p g c", g=PASSES)[:, passes, cols]
            h_t = gated_of[m][:].rearrange("p (g c) -> p g c", g=PASSES)[:, passes, cols]
            z = psum_of["gates"].tile([P, K_PASS], F32, name="z")
            nc.tensor.matmul(
                out=z[:].rearrange("p (g c) -> p g c", g=2), lhsT=wg_t[:], rhs=a_t, start=True, stop=True
            )
            gate = gate_pool.tile([P, K_PASS], F32, name="gate")
            nc.scalar.activation(out=gate[:], in_=z[:], func=SIGMOID, bias=bg_col[:, 0:1])
            nc.vector.tensor_tensor(out=h_t, in0=gate[:].rearrange("p (g c) -> p g c", g=2), in1=a_t, op=MULT)

        def gate_half(m, i):
            for j in range(PASSES // 2):
                gate_tokens(m, i, j)

        def quantise_tokens(m):
            nc.vector.quantize_mx(
                out=h_codes[:, m, :].bitcast(FP8X4), scales=h_scales[:, m, :], in_=gated_of[m][:]
            )

        def transpose_wo(s):
            grouped_of[s] = grouped_pool.tile([P, PASSES * SLAB * PACK], BF16, name="grouped", align_bytes=64)
            transpose_rows(wo_in[:, s, :, :], BLOCK_BANKS, grouped_of[s], False)

        def quantise_wo(s):
            cols = slice(s * SLAB, (s + 1) * SLAB)
            for g in range(PASSES):
                nc.vector.quantize_mx(
                    out=wo_codes[:, g, cols].bitcast(FP8X4),
                    scales=wo_scales[:, g, cols],
                    in_=grouped_of[s][:, g * SLAB * PACK : (g + 1) * SLAB * PACK],
                )

        def product(m, n):
            cols = slice(n * CHUNK, (n + 1) * CHUNK)
            acc = psum_of["products"].tile([P, CHUNK], F32, name="acc")
            for g in range(PASSES):
                toks = slice(g * P, (g + 1) * P)
                nc.tensor.matmul_mx(
                    out=acc[:],
                    lhsT=h_codes[:, m, toks].bitcast(FP8X4),
                    lhsT_scale=h_scales[:, m, toks],
                    rhs=wo_codes[:, g, cols].bitcast(FP8X4),
                    rhs_scale=wo_scales[:, g, cols],
                    start=(g == 0),
                    stop=(g == PASSES - 1),
                )
            result = result_pool.tile([P, CHUNK], F32, name="result")
            nc.vector.tensor_tensor(out=result[:], in0=acc[:], in1=bo_all[:, cols], op=ADD)
            nc.sync.dma_start(out=out_rows[m * P : (m + 1) * P, cols], in_=result[:])

        with ExitStack() as early:
            divide_psum(early, "early_", BLOCK_BANKS, 2, 2)

            transpose_tokens(0)
            set_up_gate()
            for m in range(FIRST):
                gate_half(m, 0)
                if m > 0:
                    quantise_tokens(m - 1)
                if m + 1 < FIRST:
                    transpose_tokens(m + 1)
                gate_half(m, 1)

            for s in range(SLABS):
                transpose_wo(s)
                if s == 0:
                    quantise_tokens(FIRST - 1)
                if s >= CHUNK_SLABS:
                    for i in range(SLAB_PRODUCTS):
                        product((s % CHUNK_SLABS) * SLAB_PRODUCTS + i, s // CHUNK_SLABS - 1)
                quantise_wo(s)

        with ExitStack() as late:
            divide_psum(late, "late_", TILE_BANKS, 3, 3)

            transpose_tokens(FIRST)
            ready = [(m, CHUNKS - 1) for m in range(FIRST)]
            for m in range(FIRST, TOKEN_TILES):
                gate_half(m, 0)
                product(*ready[0])
                gate_half(m, 1)
                product(*ready[1])
                if m + 1 < TOKEN_TILES:
                    transpose_tokens(m + 1)
                product(*ready[2])
                quantise_tokens(m)
                product(*ready[3])
                ready = [(m, n) for n in range(CHUNKS)]
            for m, n in ready:
                product(m, n)
